import numpy as np
import ml_dtypes


def mxq(x, axis, fmt="e4m3"):
    dtype, down = {"e4m3": (ml_dtypes.float8_e4m3fn, 7), "e5m2": (ml_dtypes.float8_e5m2, 14)}[fmt]
    v = np.moveaxis(np.asarray(x, np.float32).astype(ml_dtypes.bfloat16).astype(np.float64), axis, -1)
    blocks = v.reshape(v.shape[:-1] + (-1, 32))
    amax = np.abs(blocks).max(-1, keepdims=True)
    byte = np.maximum(np.where(amax > 0, np.frexp(amax)[1] - 1 + 127, 0) - down, 1)
    scale = np.exp2(byte - 127.0)
    codes = (blocks / scale).astype(np.float32).astype(dtype).astype(np.float64)
    return np.moveaxis((codes * scale).reshape(v.shape), -1, axis)


WIDE = False


def mx_kscale(k):
    if not WIDE:
        return np.ones(k)
    levels = np.array([10, -10, 5, -5, 0])
    a = np.random.permutation(np.resize(levels, k // 512 * 4)).reshape(k // 512, 4)
    idx = np.arange(k)
    return np.exp2(a[idx // 512, idx % 128 // 32])


BF16 = ml_dtypes.bfloat16


def bf(x):
    return np.asarray(x, np.float32).astype(BF16)


def f64(x):
    return np.asarray(x).astype(np.float64)


B, D, H, O = 2048, 512, 512, 512


def silu(v):
    with np.errstate(over="ignore"):
        return v / (1.0 + np.exp(-v))


def setup_inputs():
    s = mx_kscale(H)
    u = s / s.min()
    return {"t": bf(np.random.random(B)),
            "W1": bf(np.random.standard_normal((H, D)) * 2.0 / np.sqrt(D) * u[:, None]),
            "b1": bf(np.random.standard_normal(H) * 0.5 * u),
            "W2": bf(np.random.standard_normal((O, H)) * 1.5 / np.sqrt(H) / u[None, :]),
            "b2": bf(np.random.standard_normal(O) * 0.5)}


def reference(t, W1, b1, W2, b2):
    t = f64(t)
    phase = (np.arange(D, dtype=np.float64) / D) * np.pi
    tb = t[:, None]
    emb = tb * np.cos(phase[None, :] * tb) + tb * np.sin(phase[None, :] * (1.0 - tb))
    x = silu((mxq(emb, 1, "e4m3") @ mxq(f64(W1), 1, "e4m3").T) + f64(b1))
    x = silu((mxq(x, 1, "e4m3") @ mxq(f64(W2), 1, "e4m3").T) + f64(b2))
    return x

@@ -1,0 +1,247 @@
+import math
+from contextlib import ExitStack
+
+import concourse.mybir as mybir
+from concourse.masks import make_identity
+
+F32 = mybir.dt.float32
+BF16 = mybir.dt.bfloat16
+I32 = mybir.dt.int32
+U32 = mybir.dt.uint32
+U8 = mybir.dt.uint8
+FP8X4 = mybir.dt.float8_e4m3fn_x4
+ACT = mybir.ActivationFunctionType
+ALU = mybir.AluOpType
+
+P = 128
+B, D, H, O = 2048, 512, 512, 512
+NB = 512
+CH = B // NB
+FLOPS = 2 * B * D * H + 2 * B * H * O
+
+AMP_ON_GPSIMD = True
+REGROUP_ON_GPSIMD = False
+
+
+def tile_input_timestep_kernel(tc, t, W1, b1, W2, b2, out):
+    nc = tc.nc
+    with ExitStack() as ctx:
+        keep = ctx.enter_context(tc.tile_pool(name="keep", bufs=1))
+        psum = ctx.enter_context(tc.psum_pool(name="psum", bufs=4))
+        ctx.enter_context(tc.manual_schedule())
+
+        t_row = keep.tile([P, B], BF16, name="t_row")
+        nc.vector.memset(t_row[:].bitcast(I32), 0)
+        nc.sync.dma_start(out=t_row[0:1, :], in_=t.rearrange("(o b) -> o b", o=1))
+        w1_raw = keep.tile([P, 4, D], BF16, name="w1_raw")
+        nc.sync.dma_start(out=w1_raw[:], in_=W1.rearrange("(p t) d -> p t d", t=4))
+        w2_raw = keep.tile([P, 4, H], BF16, name="w2_raw")
+        nc.sync.dma_start(out=w2_raw[:], in_=W2.rearrange("(c p) h -> p c h", p=P))
+        b1_raw = keep.tile([P, 4], BF16, name="b1_raw")
+        nc.scalar.dma_start(out=b1_raw[:], in_=b1.rearrange("(p t) -> p t", t=4))
+        b2_all = keep.tile([P, O], BF16, name="b2_all")
+        nc.scalar.dma_start(out=b2_all[:], in_=b2.partition_broadcast(P))
+
+        ones = keep.tile([P, P], BF16, name="ones")
+        nc.vector.memset(ones[:], 1.0)
+        index = keep.tile([P, 4], I32, name="index")
+        nc.gpsimd.iota(index[:], pattern=[[1, 4]], base=0, channel_multiplier=4)
+        ident = keep.tile([P, P], F32, name="ident")
+        make_identity(nc, ident[:])
+        neg_a = keep.tile([P, 4], F32, name="neg_a")
+        nc.vector.tensor_scalar(out=neg_a[:], in0=index[:], scalar1=-math.pi / D, scalar2=None, op0=ALU.mult)
+        shift = keep.tile([P, 4], F32, name="shift")
+        nc.vector.tensor_scalar(
+            out=shift[:], in0=index[:], scalar1=math.pi / (2 * D), scalar2=math.pi / 4, op0=ALU.mult, op1=ALU.add
+        )
+        half_amp = keep.tile([P, 4], F32, name="half_amp")
+        nc.scalar.activation(out=half_amp[:], in_=shift[:], func=ACT.Sin)
+
+        t_all = []
+        for c in range(CH):
+            bank = psum.tile([P, NB], F32, name="t_all%d" % c, tag="A")
+            nc.tensor.matmul(out=bank[:], lhsT=ones[:], rhs=t_row[:, c * NB : (c + 1) * NB], start=True, stop=True)
+            t_all.append(bank)
+
+        def transpose_weight(raw, label):
+            banks = []
+            for half in range(2):
+                bank = psum.tile([P, 2, 2, P], F32, name="%s_t%d" % (label, half), tag="B")
+                for r in range(2):
+                    words = raw[:, 2 * half + r, :].bitcast(F32).rearrange("p (q u) -> p u q", u=2)
+                    for u in range(2):
+                        nc.tensor.transpose(out=bank[:, r, u, :], in_=words[:, u, :], identity=ident[:])
+                banks.append(bank)
+            return banks
+
+        w1_banks = transpose_weight(w1_raw, "w1")
+        w2_banks = transpose_weight(w2_raw, "w2")
+
+        def empty_weight(banks, label):
+            grouped = keep.tile([P, 4 * P * 4], BF16, name="%s_grouped" % label, align_bytes=64)
+            words = grouped[:].bitcast(F32).rearrange("p (r m u) -> p r m u", r=4, u=2)
+            for half in range(2):
+                nc.vector.tensor_copy(
+                    out=words[:, 2 * half : 2 * half + 2], in_=banks[half][:].rearrange("p r u m -> p r m u")
+                )
+            return grouped
+
+        def quantise(src_flat, label):
+            codes = keep.tile([P, 512], U32, name="%s_codes" % label, align_bytes=64)
+            scales = keep.tile([P, 512], U8, name="%s_scales" % label, align_bytes=64)
+            nc.vector.quantize_mx(out=codes[:].bitcast(FP8X4), scales=scales[:], in_=src_flat)
+            return codes, scales
+
+        sines = []
+
+        def sine(c):
+            s = keep.tile([P, 4, NB], F32, name="sine%d" % c)
+            for j in range(4):
+                nc.scalar.activation(
+                    out=s[:, j, :], in_=t_all[c][:], func=ACT.Sin, bias=shift[:, j : j + 1], scale=neg_a[:, j : j + 1]
+                )
+            for j in range(4):
+                eng = nc.gpsimd if AMP_ON_GPSIMD else nc.vector
+                eng.tensor_scalar(
+                    out=s[:, j, :], in0=s[:, j, :], scalar1=half_amp[:, j : j + 1], scalar2=2.0, op0=ALU.mult, op1=ALU.mult
+                )
+            sines.append(s)
+
+        emb = {}
+
+        def times_t(c):
+            e = keep.tile([P, NB, 4], BF16, name="emb%d" % c, align_bytes=64)
+            nc.vector.tensor_tensor(
+                out=e[:],
+                in0=sines[c][:].rearrange("p j b -> p b j"),
+                in1=t_all[c][:].unsqueeze(2).to_broadcast([P, NB, 4]),
+                op=ALU.mult,
+            )
+            emb[c] = e
+
+        emb_q = {}
+
+        def quantise_emb(c):
+            emb_q[c] = quantise(emb[c][:].rearrange("p b j -> p (b j)"), "emb%d" % c)
+
+        z = {}
+
+        def layer1(c, r):
+            bank = psum.tile([P, NB], F32, name="z%d_%d" % (c, r), tag=("B" if c == 0 else "A"))
+            cols = slice(r * P, (r + 1) * P)
+            nc.tensor.matmul_mx(
+                out=bank[:],
+                lhsT=w1_q[0][:, cols].bitcast(FP8X4),
+                lhsT_scale=w1_q[1][:, cols],
+                rhs=emb_q[c][0][:].bitcast(FP8X4),
+                rhs_scale=emb_q[c][1][:],
+                start=True,
+                stop=True,
+            )
+            z[(c, r)] = bank
+
+        h_planes = {}
+
+        def silu1(c):
+            hp = keep.tile([P, 4, NB], BF16, name="h_planes%d" % c)
+            for r in range(4):
+                nc.scalar.activation(out=hp[:, r, :], in_=z[(c, r)][:], func=ACT.Silu, bias=b1_f[:, r : r + 1], scale=1.0)
+            h_planes[c] = hp
+
+        h_grouped = {}
+
+        def regroup(c):
+            hg = keep.tile([P, NB, 4], BF16, name="h_grouped%d" % c, align_bytes=64)
+            dst = hg[:].rearrange("p (c i) r -> p c r i", i=4)
+            src = h_planes[c][:].rearrange("p r (c i) -> p c r i", i=4)
+            if REGROUP_ON_GPSIMD:
+                nc.gpsimd.tensor_scalar(out=dst, in0=src, scalar1=1.0, scalar2=0.0, op0=ALU.mult, op1=ALU.add)
+            else:
+                nc.vector.tensor_copy(out=dst, in_=src)
+            h_grouped[c] = hg
+
+        h_q = {}
+
+        def quantise_h(c):
+            h_q[c] = quantise(h_grouped[c][:].rearrange("p b r -> p (b r)"), "h%d" % c)
+
+        v = {}
+
+        def layer2(c):
+            for s in range(4):
+                bank = psum.tile([P, O], F32, name="v%d_%d" % (c, s), tag="B")
+                cols = slice(s * P, (s + 1) * P)
+                nc.tensor.matmul_mx(
+                    out=bank[:],
+                    lhsT=h_q[c][0][:, cols].bitcast(FP8X4),
+                    lhsT_scale=h_q[c][1][:, cols],
+                    rhs=w2_q[0][:].bitcast(FP8X4),
+                    rhs_scale=w2_q[1][:],
+                    start=True,
+                    stop=True,
+                )
+                v[(c, s)] = bank
+
+        y = {}
+
+        def add_bias2(c):
+            yt = keep.tile([P, 4, O], F32, name="y%d" % c)
+            for s in range(4):
+                nc.vector.tensor_tensor(out=yt[:, s, :], in0=v[(c, s)][:], in1=b2_all[:], op=ALU.add)
+            y[c] = yt
+
+        def silu2_store(c):
+            for s in range(4):
+                nc.scalar.activation(out=y[c][:, s, :], in_=y[c][:, s, :], func=ACT.Silu)
+                row = c * NB + s * P
+                nc.sync.dma_start(out=out[row : row + P, :], in_=y[c][:, s, :])
+
+        for c in range(CH):
+            sine(c)
+        w1_grouped = empty_weight(w1_banks, "w1")
+        times_t(0)
+        w1_q = quantise(w1_grouped[:], "w1")
+        w2_grouped = empty_weight(w2_banks, "w2")
+        times_t(1)
+        w2_q = quantise(w2_grouped[:], "w2")
+        quantise_emb(0)
+        for r in range(4):
+            layer1(0, r)
+        times_t(2)
+        quantise_emb(1)
+        for r in range(3):
+            layer1(1, r)
+        b1_f = keep.tile([P, 4], F32, name="b1_f")
+        nc.vector.tensor_copy(out=b1_f[:], in_=b1_raw[:])
+        silu1(0)
+        times_t(3)
+        layer1(1, 3)
+        quantise_emb(2)
+        silu1(1)
+        for r in range(4):
+            layer1(2, r)
+        regroup(0)
+        quantise_emb(3)
+        quantise_h(0)
+        layer2(0)
+        silu1(2)
+        for r in range(4):
+            layer1(3, r)
+        regroup(1)
+        add_bias2(0)
+        silu2_store(0)
+        silu1(3)
+        quantise_h(1)
+        layer2(1)
+        regroup(2)
+        add_bias2(1)
+        silu2_store(1)
+        quantise_h(2)
+        layer2(2)
+        regroup(3)
+        add_bias2(2)
+        silu2_store(2)
+        quantise_h(3)
+        layer2(3)
+        add_bias2(3)
+        silu2_store(3)

@@ -19,9 +19,6 @@ NB = 512
 CH = B // NB
 FLOPS = 2 * B * D * H + 2 * B * H * O
 
-AMP_ON_GPSIMD = True
-REGROUP_ON_GPSIMD = False
-
 
 def tile_input_timestep_kernel(tc, t, W1, b1, W2, b2, out):
     nc = tc.nc
@@ -38,9 +35,9 @@ def tile_input_timestep_kernel(tc, t, W1, b1, W2, b2, out):
         w2_raw = keep.tile([P, 4, H], BF16, name="w2_raw")
         nc.sync.dma_start(out=w2_raw[:], in_=W2.rearrange("(c p) h -> p c h", p=P))
         b1_raw = keep.tile([P, 4], BF16, name="b1_raw")
-        nc.scalar.dma_start(out=b1_raw[:], in_=b1.rearrange("(p t) -> p t", t=4))
+        nc.sync.dma_start(out=b1_raw[:], in_=b1.rearrange("(p t) -> p t", t=4))
         b2_all = keep.tile([P, O], BF16, name="b2_all")
-        nc.scalar.dma_start(out=b2_all[:], in_=b2.partition_broadcast(P))
+        nc.sync.dma_start(out=b2_all[:], in_=b2.partition_broadcast(P))
 
         ones = keep.tile([P, P], BF16, name="ones")
         nc.vector.memset(ones[:], 1.0)
@@ -56,6 +53,8 @@ def tile_input_timestep_kernel(tc, t, W1, b1, W2, b2, out):
         )
         half_amp = keep.tile([P, 4], F32, name="half_amp")
         nc.scalar.activation(out=half_amp[:], in_=shift[:], func=ACT.Sin)
+        amp = keep.tile([P, 4], F32, name="amp")
+        nc.vector.tensor_scalar(out=amp[:], in0=half_amp[:], scalar1=2.0, scalar2=None, op0=ALU.mult)
 
         t_all = []
         for c in range(CH):
@@ -81,9 +80,7 @@ def tile_input_timestep_kernel(tc, t, W1, b1, W2, b2, out):
             grouped = keep.tile([P, 4 * P * 4], BF16, name="%s_grouped" % label, align_bytes=64)
             words = grouped[:].bitcast(F32).rearrange("p (r m u) -> p r m u", r=4, u=2)
             for half in range(2):
-                nc.vector.tensor_copy(
-                    out=words[:, 2 * half : 2 * half + 2], in_=banks[half][:].rearrange("p r u m -> p r m u")
-                )
+                nc.scalar.copy(out=words[:, 2 * half : 2 * half + 2], in_=banks[half][:].rearrange("p r u m -> p r m u"))
             return grouped
 
         def quantise(src_flat, label):
@@ -100,24 +97,29 @@ def tile_input_timestep_kernel(tc, t, W1, b1, W2, b2, out):
                 nc.scalar.activation(
                     out=s[:, j, :], in_=t_all[c][:], func=ACT.Sin, bias=shift[:, j : j + 1], scale=neg_a[:, j : j + 1]
                 )
-            for j in range(4):
-                eng = nc.gpsimd if AMP_ON_GPSIMD else nc.vector
-                eng.tensor_scalar(
-                    out=s[:, j, :], in0=s[:, j, :], scalar1=half_amp[:, j : j + 1], scalar2=2.0, op0=ALU.mult, op1=ALU.mult
-                )
             sines.append(s)
+
+        emb_planes = {}
+
+        def times_amp_t(c):
+            ep = keep.tile([P, 4, NB], BF16, name="emb_planes%d" % c)
+            for j in range(4):
+                nc.vector.scalar_tensor_tensor(
+                    out=ep[:, j, :], in0=sines[c][:, j, :], scalar=amp[:, j : j + 1], in1=t_all[c][:], op0=ALU.mult, op1=ALU.mult
+                )
+            emb_planes[c] = ep
+
+        def side_by_side(planes, label):
+            grouped = keep.tile([P, NB, 4], BF16, name=label, align_bytes=64)
+            nc.vector.tensor_copy(
+                out=grouped[:].rearrange("p (c i) r -> p c r i", i=4), in_=planes[:].rearrange("p r (c i) -> p c r i", i=4)
+            )
+            return grouped
 
         emb = {}
 
-        def times_t(c):
-            e = keep.tile([P, NB, 4], BF16, name="emb%d" % c, align_bytes=64)
-            nc.vector.tensor_tensor(
-                out=e[:],
-                in0=sines[c][:].rearrange("p j b -> p b j"),
-                in1=t_all[c][:].unsqueeze(2).to_broadcast([P, NB, 4]),
-                op=ALU.mult,
-            )
-            emb[c] = e
+        def regroup_emb(c):
+            emb[c] = side_by_side(emb_planes[c], "emb%d" % c)
 
         emb_q = {}
 
@@ -151,14 +153,7 @@ def tile_input_timestep_kernel(tc, t, W1, b1, W2, b2, out):
         h_grouped = {}
 
         def regroup(c):
-            hg = keep.tile([P, NB, 4], BF16, name="h_grouped%d" % c, align_bytes=64)
-            dst = hg[:].rearrange("p (c i) r -> p c r i", i=4)
-            src = h_planes[c][:].rearrange("p r (c i) -> p c r i", i=4)
-            if REGROUP_ON_GPSIMD:
-                nc.gpsimd.tensor_scalar(out=dst, in0=src, scalar1=1.0, scalar2=0.0, op0=ALU.mult, op1=ALU.add)
-            else:
-                nc.vector.tensor_copy(out=dst, in_=src)
-            h_grouped[c] = hg
+            h_grouped[c] = side_by_side(h_planes[c], "h_grouped%d" % c)
 
         h_q = {}
 
@@ -184,11 +179,11 @@ def tile_input_timestep_kernel(tc, t, W1, b1, W2, b2, out):
 
         y = {}
 
-        def add_bias2(c):
-            yt = keep.tile([P, 4, O], F32, name="y%d" % c)
-            for s in range(4):
-                nc.vector.tensor_tensor(out=yt[:, s, :], in0=v[(c, s)][:], in1=b2_all[:], op=ALU.add)
-            y[c] = yt
+        def add_bias2(c, pieces):
+            if c not in y:
+                y[c] = keep.tile([P, 4, O], F32, name="y%d" % c)
+            for s in pieces:
+                nc.vector.tensor_tensor(out=y[c][:, s, :], in0=v[(c, s)][:], in1=b2_all[:], op=ALU.add)
 
         def silu2_store(c):
             for s in range(4):
@@ -196,52 +191,60 @@ def tile_input_timestep_kernel(tc, t, W1, b1, W2, b2, out):
                 row = c * NB + s * P
                 nc.sync.dma_start(out=out[row : row + P, :], in_=y[c][:, s, :])
 
-        for c in range(CH):
-            sine(c)
+        ALL = (0, 1, 2, 3)
+        sine(0)
         w1_grouped = empty_weight(w1_banks, "w1")
-        times_t(0)
-        w1_q = quantise(w1_grouped[:], "w1")
+        sine(1)
         w2_grouped = empty_weight(w2_banks, "w2")
-        times_t(1)
-        w2_q = quantise(w2_grouped[:], "w2")
+        sine(2)
+        sine(3)
+        times_amp_t(0)
+        regroup_emb(0)
+        times_amp_t(1)
+        w1_q = quantise(w1_grouped[:], "w1")
         quantise_emb(0)
-        for r in range(4):
+        for r in ALL:
             layer1(0, r)
-        times_t(2)
-        quantise_emb(1)
-        for r in range(3):
-            layer1(1, r)
+        regroup_emb(1)
         b1_f = keep.tile([P, 4], F32, name="b1_f")
         nc.vector.tensor_copy(out=b1_f[:], in_=b1_raw[:])
+        times_amp_t(2)
+        w2_q = quantise(w2_grouped[:], "w2")
+        quantise_emb(1)
+        for r in (0, 1, 2):
+            layer1(1, r)
         silu1(0)
-        times_t(3)
+        regroup_emb(2)
+        times_amp_t(3)
         layer1(1, 3)
         quantise_emb(2)
         silu1(1)
-        for r in range(4):
+        for r in ALL:
             layer1(2, r)
+        regroup_emb(3)
         regroup(0)
         quantise_emb(3)
         quantise_h(0)
         layer2(0)
         silu1(2)
-        for r in range(4):
+        for r in ALL:
             layer1(3, r)
         regroup(1)
-        add_bias2(0)
-        silu2_store(0)
-        silu1(3)
+        add_bias2(0, ALL)
         quantise_h(1)
         layer2(1)
+        silu1(3)
         regroup(2)
-        add_bias2(1)
-        silu2_store(1)
+        add_bias2(1, ALL)
+        silu2_store(0)
         quantise_h(2)
         layer2(2)
         regroup(3)
-        add_bias2(2)
-        silu2_store(2)
+        add_bias2(2, (0,))
         quantise_h(3)
+        add_bias2(2, (1, 2, 3))
+        silu2_store(1)
         layer2(3)
-        add_bias2(3)
+        silu2_store(2)
+        add_bias2(3, ALL)
         silu2_store(3)

@@ -17,6 +17,7 @@ P = 128
 B, D, H, O = 2048, 512, 512, 512
 NB = 512
 CH = B // NB
+NF = B // P
 FLOPS = 2 * B * D * H + 2 * B * H * O
 
 
@@ -27,9 +28,8 @@ def tile_input_timestep_kernel(tc, t, W1, b1, W2, b2, out):
         psum = ctx.enter_context(tc.psum_pool(name="psum", bufs=4))
         ctx.enter_context(tc.manual_schedule())
 
-        t_row = keep.tile([P, B], BF16, name="t_row")
-        nc.vector.memset(t_row[:].bitcast(I32), 0)
-        nc.sync.dma_start(out=t_row[0:1, :], in_=t.rearrange("(o b) -> o b", o=1))
+        t_sq = keep.tile([P, NF], BF16, name="t_sq")
+        nc.sync.dma_start(out=t_sq[:], in_=t.rearrange("(n f) -> n f", f=NF))
         w1_raw = keep.tile([P, 4, D], BF16, name="w1_raw")
         nc.sync.dma_start(out=w1_raw[:], in_=W1.rearrange("(p t) d -> p t d", t=4))
         w2_raw = keep.tile([P, 4, H], BF16, name="w2_raw")
@@ -39,8 +39,6 @@ def tile_input_timestep_kernel(tc, t, W1, b1, W2, b2, out):
         b2_all = keep.tile([P, O], BF16, name="b2_all")
         nc.sync.dma_start(out=b2_all[:], in_=b2.partition_broadcast(P))
 
-        ones = keep.tile([P, P], BF16, name="ones")
-        nc.vector.memset(ones[:], 1.0)
         index = keep.tile([P, 4], I32, name="index")
         nc.gpsimd.iota(index[:], pattern=[[1, 4]], base=0, channel_multiplier=4)
         ident = keep.tile([P, P], F32, name="ident")
@@ -51,6 +49,8 @@ def tile_input_timestep_kernel(tc, t, W1, b1, W2, b2, out):
         nc.vector.tensor_scalar(
             out=shift[:], in0=index[:], scalar1=math.pi / (2 * D), scalar2=math.pi / 4, op0=ALU.mult, op1=ALU.add
         )
+        ident_bf = keep.tile([P, P], BF16, name="ident_bf")
+        nc.vector.tensor_copy(out=ident_bf[:], in_=ident[:])
         half_amp = keep.tile([P, 4], F32, name="half_amp")
         nc.scalar.activation(out=half_amp[:], in_=shift[:], func=ACT.Sin)
         amp = keep.tile([P, 4], F32, name="amp")
@@ -59,7 +59,15 @@ def tile_input_timestep_kernel(tc, t, W1, b1, W2, b2, out):
         t_all = []
         for c in range(CH):
             bank = psum.tile([P, NB], F32, name="t_all%d" % c, tag="A")
-            nc.tensor.matmul(out=bank[:], lhsT=ones[:], rhs=t_row[:, c * NB : (c + 1) * NB], start=True, stop=True)
+            for s in range(4):
+                f = 4 * c + s
+                nc.tensor.matmul(
+                    out=bank[:, s * P : (s + 1) * P],
+                    lhsT=t_sq[:, f : f + 1].to_broadcast([P, P]),
+                    rhs=ident_bf[:],
+                    start=True,
+                    stop=True,
+                )
             t_all.append(bank)
 
         def transpose_weight(raw, label):
@@ -109,17 +117,22 @@ def tile_input_timestep_kernel(tc, t, W1, b1, W2, b2, out):
                 )
             emb_planes[c] = ep
 
-        def side_by_side(planes, label):
-            grouped = keep.tile([P, NB, 4], BF16, name=label, align_bytes=64)
-            nc.vector.tensor_copy(
-                out=grouped[:].rearrange("p (c i) r -> p c r i", i=4), in_=planes[:].rearrange("p r (c i) -> p c r i", i=4)
-            )
+        def side_by_side(planes, label, on_gpsimd):
+            grouped = keep.tile([P, NB, 4], BF16, name=label, tag="grouped", align_bytes=64)
+            if on_gpsimd:
+                nc.gpsimd.tensor_scalar(
+                    out=grouped[:], in0=planes[:].rearrange("p r b -> p b r"), scalar1=1.0, scalar2=0.0, op0=ALU.mult, op1=ALU.add
+                )
+            else:
+                nc.vector.tensor_copy(
+                    out=grouped[:].rearrange("p (c i) r -> p c r i", i=4), in_=planes[:].rearrange("p r (c i) -> p c r i", i=4)
+                )
             return grouped
 
         emb = {}
 
         def regroup_emb(c):
-            emb[c] = side_by_side(emb_planes[c], "emb%d" % c)
+            emb[c] = side_by_side(emb_planes[c], "emb%d" % c, c < 3)
 
         emb_q = {}
 
@@ -153,7 +166,7 @@ def tile_input_timestep_kernel(tc, t, W1, b1, W2, b2, out):
         h_grouped = {}
 
         def regroup(c):
-            h_grouped[c] = side_by_side(h_planes[c], "h_grouped%d" % c)
+            h_grouped[c] = side_by_side(h_planes[c], "h_grouped%d" % c, c >= 2)
 
         h_q = {}
 
@@ -178,6 +191,7 @@ def tile_input_timestep_kernel(tc, t, W1, b1, W2, b2, out):
                 v[(c, s)] = bank
 
         y = {}
+        out_rows = out.rearrange("(n f) o -> n f o", f=NF)
 
         def add_bias2(c, pieces):
             if c not in y:
@@ -188,63 +202,61 @@ def tile_input_timestep_kernel(tc, t, W1, b1, W2, b2, out):
         def silu2_store(c):
             for s in range(4):
                 nc.scalar.activation(out=y[c][:, s, :], in_=y[c][:, s, :], func=ACT.Silu)
-                row = c * NB + s * P
-                nc.sync.dma_start(out=out[row : row + P, :], in_=y[c][:, s, :])
+                nc.sync.dma_start(out=out_rows[:, 4 * c + s, :], in_=y[c][:, s, :])
 
         ALL = (0, 1, 2, 3)
         sine(0)
-        w1_grouped = empty_weight(w1_banks, "w1")
         sine(1)
-        w2_grouped = empty_weight(w2_banks, "w2")
-        sine(2)
-        sine(3)
         times_amp_t(0)
         regroup_emb(0)
+        w1_grouped = empty_weight(w1_banks, "w1")
         times_amp_t(1)
-        w1_q = quantise(w1_grouped[:], "w1")
         quantise_emb(0)
+        sine(2)
+        w2_grouped = empty_weight(w2_banks, "w2")
+        sine(3)
+        w1_q = quantise(w1_grouped[:], "w1")
+        regroup_emb(1)
+        times_amp_t(2)
+        quantise_emb(1)
         for r in ALL:
             layer1(0, r)
-        regroup_emb(1)
-        b1_f = keep.tile([P, 4], F32, name="b1_f")
-        nc.vector.tensor_copy(out=b1_f[:], in_=b1_raw[:])
-        times_amp_t(2)
         w2_q = quantise(w2_grouped[:], "w2")
-        quantise_emb(1)
         for r in (0, 1, 2):
             layer1(1, r)
-        silu1(0)
-        regroup_emb(2)
         times_amp_t(3)
-        layer1(1, 3)
+        regroup_emb(2)
+        b1_f = keep.tile([P, 4], F32, name="b1_f")
+        nc.vector.tensor_copy(out=b1_f[:], in_=b1_raw[:])
         quantise_emb(2)
+        silu1(0)
+        regroup_emb(3)
+        quantise_emb(3)
+        layer1(1, 3)
         silu1(1)
         for r in ALL:
             layer1(2, r)
-        regroup_emb(3)
         regroup(0)
-        quantise_emb(3)
         quantise_h(0)
+        regroup(1)
         layer2(0)
         silu1(2)
+        quantise_h(1)
         for r in ALL:
             layer1(3, r)
-        regroup(1)
-        add_bias2(0, ALL)
-        quantise_h(1)
-        layer2(1)
         silu1(3)
-        regroup(2)
+        add_bias2(0, ALL)
+        layer2(1)
         add_bias2(1, ALL)
-        silu2_store(0)
+        regroup(2)
         quantise_h(2)
-        layer2(2)
-        regroup(3)
-        add_bias2(2, (0,))
-        quantise_h(3)
-        add_bias2(2, (1, 2, 3))
+        silu2_store(0)
         silu2_store(1)
-        layer2(3)
+        layer2(2)
+        add_bias2(2, ALL)
+        regroup(3)
+        quantise_h(3)
         silu2_store(2)
+        layer2(3)
         add_bias2(3, ALL)
         silu2_store(3)

@@ -117,22 +117,15 @@ def tile_input_timestep_kernel(tc, t, W1, b1, W2, b2, out):
                 )
             emb_planes[c] = ep
 
-        def side_by_side(planes, label, on_gpsimd):
-            grouped = keep.tile([P, NB, 4], BF16, name=label, tag="grouped", align_bytes=64)
-            if on_gpsimd:
-                nc.gpsimd.tensor_scalar(
-                    out=grouped[:], in0=planes[:].rearrange("p r b -> p b r"), scalar1=1.0, scalar2=0.0, op0=ALU.mult, op1=ALU.add
-                )
-            else:
-                nc.vector.tensor_copy(
-                    out=grouped[:].rearrange("p (c i) r -> p c r i", i=4), in_=planes[:].rearrange("p r (c i) -> p c r i", i=4)
-                )
+        def side_by_side(planes, label, engine_copy):
+            grouped = keep.tile([P, NB, 4], BF16, name=label, align_bytes=64)
+            engine_copy(out=grouped[:].rearrange("p (c i) r -> p c r i", i=4), in_=planes[:].rearrange("p r (c i) -> p c r i", i=4))
             return grouped
 
         emb = {}
 
         def regroup_emb(c):
-            emb[c] = side_by_side(emb_planes[c], "emb%d" % c, c < 3)
+            emb[c] = side_by_side(emb_planes[c], "emb%d" % c, nc.vector.tensor_copy)
 
         emb_q = {}
 
@@ -166,7 +159,7 @@ def tile_input_timestep_kernel(tc, t, W1, b1, W2, b2, out):
         h_grouped = {}
 
         def regroup(c):
-            h_grouped[c] = side_by_side(h_planes[c], "h_grouped%d" % c, c >= 2)
+            h_grouped[c] = side_by_side(h_planes[c], "h_grouped%d" % c, nc.scalar.copy if c == 3 else nc.vector.tensor_copy)
 
         h_q = {}
 
@@ -207,56 +200,57 @@ def tile_input_timestep_kernel(tc, t, W1, b1, W2, b2, out):
         ALL = (0, 1, 2, 3)
         sine(0)
         sine(1)
-        times_amp_t(0)
-        regroup_emb(0)
         w1_grouped = empty_weight(w1_banks, "w1")
-        times_amp_t(1)
-        quantise_emb(0)
         sine(2)
         w2_grouped = empty_weight(w2_banks, "w2")
         sine(3)
-        w1_q = quantise(w1_grouped[:], "w1")
+        times_amp_t(0)
+        regroup_emb(0)
+        times_amp_t(1)
+        quantise_emb(0)
         regroup_emb(1)
-        times_amp_t(2)
-        quantise_emb(1)
+        w1_q = quantise(w1_grouped[:], "w1")
         for r in ALL:
             layer1(0, r)
-        w2_q = quantise(w2_grouped[:], "w2")
-        for r in (0, 1, 2):
-            layer1(1, r)
-        times_amp_t(3)
+        times_amp_t(2)
+        quantise_emb(1)
         regroup_emb(2)
+        w2_q = quantise(w2_grouped[:], "w2")
         b1_f = keep.tile([P, 4], F32, name="b1_f")
         nc.vector.tensor_copy(out=b1_f[:], in_=b1_raw[:])
-        quantise_emb(2)
+        for r in (0, 1, 2):
+            layer1(1, r)
         silu1(0)
+        times_amp_t(3)
+        for r in (3,):
+            layer1(1, r)
+        quantise_emb(2)
         regroup_emb(3)
-        quantise_emb(3)
-        layer1(1, 3)
         silu1(1)
         for r in ALL:
             layer1(2, r)
         regroup(0)
-        quantise_h(0)
-        regroup(1)
-        layer2(0)
+        quantise_emb(3)
         silu1(2)
-        quantise_h(1)
         for r in ALL:
             layer1(3, r)
+        regroup(1)
+        quantise_h(0)
+        layer2(0)
         silu1(3)
+        regroup(2)
+        quantise_h(1)
         add_bias2(0, ALL)
         layer2(1)
-        add_bias2(1, ALL)
-        regroup(2)
-        quantise_h(2)
-        silu2_store(0)
-        silu2_store(1)
-        layer2(2)
-        add_bias2(2, ALL)
         regroup(3)
+        quantise_h(2)
+        add_bias2(1, ALL)
+        layer2(2)
+        silu2_store(0)
         quantise_h(3)
-        silu2_store(2)
+        add_bias2(2, ALL)
         layer2(3)
+        silu2_store(1)
         add_bias2(3, ALL)
+        silu2_store(2)
         silu2_store(3)

@@ -17,7 +17,6 @@ P = 128
 B, D, H, O = 2048, 512, 512, 512
 NB = 512
 CH = B // NB
-NF = B // P
 FLOPS = 2 * B * D * H + 2 * B * H * O
 
 
@@ -28,8 +27,15 @@ def tile_input_timestep_kernel(tc, t, W1, b1, W2, b2, out):
         psum = ctx.enter_context(tc.psum_pool(name="psum", bufs=4))
         ctx.enter_context(tc.manual_schedule())
 
-        t_sq = keep.tile([P, NF], BF16, name="t_sq")
-        nc.sync.dma_start(out=t_sq[:], in_=t.rearrange("(n f) -> n f", f=NF))
+        t_view = t.rearrange("(o b) -> o b", o=1)
+        t_first = keep.tile([P, NB], BF16, name="t_first")
+        nc.vector.memset(t_first[:].bitcast(I32), 0)
+        nc.sync.dma_start(out=t_first[0:1, :], in_=t_view[:, 0:NB])
+        ones = keep.tile([P, P], BF16, name="ones")
+        nc.vector.memset(ones[:], 1.0)
+        t_rest = keep.tile([P, B - NB], BF16, name="t_rest")
+        nc.vector.memset(t_rest[:].bitcast(I32), 0)
+        nc.sync.dma_start(out=t_rest[0:1, :], in_=t_view[:, NB:B])
         w1_raw = keep.tile([P, 4, D], BF16, name="w1_raw")
         nc.sync.dma_start(out=w1_raw[:], in_=W1.rearrange("(p t) d -> p t d", t=4))
         w2_raw = keep.tile([P, 4, H], BF16, name="w2_raw")
@@ -49,8 +55,6 @@ def tile_input_timestep_kernel(tc, t, W1, b1, W2, b2, out):
         nc.vector.tensor_scalar(
             out=shift[:], in0=index[:], scalar1=math.pi / (2 * D), scalar2=math.pi / 4, op0=ALU.mult, op1=ALU.add
         )
-        ident_bf = keep.tile([P, P], BF16, name="ident_bf")
-        nc.vector.tensor_copy(out=ident_bf[:], in_=ident[:])
         half_amp = keep.tile([P, 4], F32, name="half_amp")
         nc.scalar.activation(out=half_amp[:], in_=shift[:], func=ACT.Sin)
         amp = keep.tile([P, 4], F32, name="amp")
@@ -59,16 +63,12 @@ def tile_input_timestep_kernel(tc, t, W1, b1, W2, b2, out):
         t_all = []
         for c in range(CH):
             bank = psum.tile([P, NB], F32, name="t_all%d" % c, tag="A")
-            for s in range(4):
-                f = 4 * c + s
-                nc.tensor.matmul(
-                    out=bank[:, s * P : (s + 1) * P],
-                    lhsT=t_sq[:, f : f + 1].to_broadcast([P, P]),
-                    rhs=ident_bf[:],
-                    start=True,
-                    stop=True,
-                )
+            rows = t_first[:] if c == 0 else t_rest[:, (c - 1) * NB : c * NB]
+            nc.tensor.matmul(out=bank[:], lhsT=ones[:], rhs=rows, start=True, stop=True)
             t_all.append(bank)
+            if c == 0:
+                t_twin = psum.tile([P, NB], F32, name="t_twin", tag="B")
+                nc.tensor.matmul(out=t_twin[:], lhsT=ones[:], rhs=rows, start=True, stop=True)
 
         def transpose_weight(raw, label):
             banks = []
@@ -82,7 +82,6 @@ def tile_input_timestep_kernel(tc, t, W1, b1, W2, b2, out):
             return banks
 
         w1_banks = transpose_weight(w1_raw, "w1")
-        w2_banks = transpose_weight(w2_raw, "w2")
 
         def empty_weight(banks, label):
             grouped = keep.tile([P, 4 * P * 4], BF16, name="%s_grouped" % label, align_bytes=64)
@@ -111,21 +110,24 @@ def tile_input_timestep_kernel(tc, t, W1, b1, W2, b2, out):
 
         def times_amp_t(c):
             ep = keep.tile([P, 4, NB], BF16, name="emb_planes%d" % c)
+            t_for_vector = t_twin if c == 0 else t_all[c]
             for j in range(4):
                 nc.vector.scalar_tensor_tensor(
-                    out=ep[:, j, :], in0=sines[c][:, j, :], scalar=amp[:, j : j + 1], in1=t_all[c][:], op0=ALU.mult, op1=ALU.mult
+                    out=ep[:, j, :], in0=sines[c][:, j, :], scalar=amp[:, j : j + 1], in1=t_for_vector[:], op0=ALU.mult, op1=ALU.mult
                 )
             emb_planes[c] = ep
 
-        def side_by_side(planes, label, engine_copy):
+        def side_by_side(planes, label):
             grouped = keep.tile([P, NB, 4], BF16, name=label, align_bytes=64)
-            engine_copy(out=grouped[:].rearrange("p (c i) r -> p c r i", i=4), in_=planes[:].rearrange("p r (c i) -> p c r i", i=4))
+            nc.vector.tensor_copy(
+                out=grouped[:].rearrange("p (c i) r -> p c r i", i=4), in_=planes[:].rearrange("p r (c i) -> p c r i", i=4)
+            )
             return grouped
 
         emb = {}
 
         def regroup_emb(c):
-            emb[c] = side_by_side(emb_planes[c], "emb%d" % c, nc.vector.tensor_copy)
+            emb[c] = side_by_side(emb_planes[c], "emb%d" % c)
 
         emb_q = {}
 
@@ -159,7 +161,7 @@ def tile_input_timestep_kernel(tc, t, W1, b1, W2, b2, out):
         h_grouped = {}
 
         def regroup(c):
-            h_grouped[c] = side_by_side(h_planes[c], "h_grouped%d" % c, nc.scalar.copy if c == 3 else nc.vector.tensor_copy)
+            h_grouped[c] = side_by_side(h_planes[c], "h_grouped%d" % c)
 
         h_q = {}
 
@@ -184,7 +186,6 @@ def tile_input_timestep_kernel(tc, t, W1, b1, W2, b2, out):
                 v[(c, s)] = bank
 
         y = {}
-        out_rows = out.rearrange("(n f) o -> n f o", f=NF)
 
         def add_bias2(c, pieces):
             if c not in y:
@@ -195,62 +196,64 @@ def tile_input_timestep_kernel(tc, t, W1, b1, W2, b2, out):
         def silu2_store(c):
             for s in range(4):
                 nc.scalar.activation(out=y[c][:, s, :], in_=y[c][:, s, :], func=ACT.Silu)
-                nc.sync.dma_start(out=out_rows[:, 4 * c + s, :], in_=y[c][:, s, :])
+                row = c * NB + s * P
+                nc.sync.dma_start(out=out[row : row + P, :], in_=y[c][:, s, :])
 
         ALL = (0, 1, 2, 3)
         sine(0)
-        sine(1)
         w1_grouped = empty_weight(w1_banks, "w1")
-        sine(2)
+        w2_banks = transpose_weight(w2_raw, "w2")
+        sine(1)
         w2_grouped = empty_weight(w2_banks, "w2")
+        sine(2)
         sine(3)
         times_amp_t(0)
         regroup_emb(0)
         times_amp_t(1)
-        quantise_emb(0)
-        regroup_emb(1)
         w1_q = quantise(w1_grouped[:], "w1")
+        quantise_emb(0)
         for r in ALL:
             layer1(0, r)
-        times_amp_t(2)
-        quantise_emb(1)
-        regroup_emb(2)
-        w2_q = quantise(w2_grouped[:], "w2")
+        regroup_emb(1)
         b1_f = keep.tile([P, 4], F32, name="b1_f")
         nc.vector.tensor_copy(out=b1_f[:], in_=b1_raw[:])
+        times_amp_t(2)
+        w2_q = quantise(w2_grouped[:], "w2")
+        quantise_emb(1)
         for r in (0, 1, 2):
             layer1(1, r)
         silu1(0)
+        regroup_emb(2)
         times_amp_t(3)
         for r in (3,):
             layer1(1, r)
         quantise_emb(2)
-        regroup_emb(3)
         silu1(1)
         for r in ALL:
             layer1(2, r)
+        regroup_emb(3)
         regroup(0)
         quantise_emb(3)
+        quantise_h(0)
+        layer2(0)
         silu1(2)
         for r in ALL:
             layer1(3, r)
         regroup(1)
-        quantise_h(0)
-        layer2(0)
+        add_bias2(0, ALL)
+        quantise_h(1)
+        layer2(1)
         silu1(3)
         regroup(2)
-        quantise_h(1)
-        add_bias2(0, ALL)
-        layer2(1)
-        regroup(3)
-        quantise_h(2)
         add_bias2(1, ALL)
-        layer2(2)
         silu2_store(0)
+        quantise_h(2)
+        layer2(2)
+        regroup(3)
         quantise_h(3)
         add_bias2(2, ALL)
-        layer2(3)
         silu2_store(1)
-        add_bias2(3, ALL)
+        layer2(3)
         silu2_store(2)
+        add_bias2(3, ALL)
         silu2_store(3)

import math
from contextlib import ExitStack

import concourse.mybir as mybir
from concourse.masks import make_identity

F32 = mybir.dt.float32
BF16 = mybir.dt.bfloat16
I32 = mybir.dt.int32
U32 = mybir.dt.uint32
U8 = mybir.dt.uint8
FP8X4 = mybir.dt.float8_e4m3fn_x4
ACT = mybir.ActivationFunctionType
ALU = mybir.AluOpType

P = 128
B, D, H, O = 2048, 512, 512, 512
NB = 512
CH = B // NB
FLOPS = 2 * B * D * H + 2 * B * H * O


def tile_input_timestep_kernel(tc, t, W1, b1, W2, b2, out):
    nc = tc.nc
    with ExitStack() as ctx:
        keep = ctx.enter_context(tc.tile_pool(name="keep", bufs=1))
        psum = ctx.enter_context(tc.psum_pool(name="psum", bufs=4))
        ctx.enter_context(tc.manual_schedule())

        t_view = t.rearrange("(o b) -> o b", o=1)
        t_first = keep.tile([P, NB], BF16, name="t_first")
        nc.vector.memset(t_first[:].bitcast(I32), 0)
        nc.sync.dma_start(out=t_first[0:1, :], in_=t_view[:, 0:NB])
        ones = keep.tile([P, P], BF16, name="ones")
        nc.vector.memset(ones[:], 1.0)
        t_rest = keep.tile([P, B - NB], BF16, name="t_rest")
        nc.vector.memset(t_rest[:].bitcast(I32), 0)
        nc.sync.dma_start(out=t_rest[0:1, :], in_=t_view[:, NB:B])
        w1_raw = keep.tile([P, 4, D], BF16, name="w1_raw")
        nc.sync.dma_start(out=w1_raw[:], in_=W1.rearrange("(p t) d -> p t d", t=4))
        w2_raw = keep.tile([P, 4, H], BF16, name="w2_raw")
        nc.sync.dma_start(out=w2_raw[:], in_=W2.rearrange("(c p) h -> p c h", p=P))
        b1_raw = keep.tile([P, 4], BF16, name="b1_raw")
        nc.sync.dma_start(out=b1_raw[:], in_=b1.rearrange("(p t) -> p t", t=4))
        b2_all = keep.tile([P, O], BF16, name="b2_all")
        nc.sync.dma_start(out=b2_all[:], in_=b2.partition_broadcast(P))

        index = keep.tile([P, 4], I32, name="index")
        nc.gpsimd.iota(index[:], pattern=[[1, 4]], base=0, channel_multiplier=4)
        ident = keep.tile([P, P], F32, name="ident")
        make_identity(nc, ident[:])
        neg_a = keep.tile([P, 4], F32, name="neg_a")
        nc.vector.tensor_scalar(out=neg_a[:], in0=index[:], scalar1=-math.pi / D, scalar2=None, op0=ALU.mult)
        shift = keep.tile([P, 4], F32, name="shift")
        nc.vector.tensor_scalar(
            out=shift[:], in0=index[:], scalar1=math.pi / (2 * D), scalar2=math.pi / 4, op0=ALU.mult, op1=ALU.add
        )
        half_amp = keep.tile([P, 4], F32, name="half_amp")
        nc.scalar.activation(out=half_amp[:], in_=shift[:], func=ACT.Sin)
        amp = keep.tile([P, 4], F32, name="amp")
        nc.vector.tensor_scalar(out=amp[:], in0=half_amp[:], scalar1=2.0, scalar2=None, op0=ALU.mult)

        t_all = []
        for c in range(CH):
            bank = psum.tile([P, NB], F32, name="t_all%d" % c, tag="A")
            rows = t_first[:] if c == 0 else t_rest[:, (c - 1) * NB : c * NB]
            nc.tensor.matmul(out=bank[:], lhsT=ones[:], rhs=rows, start=True, stop=True)
            t_all.append(bank)
            if c == 0:
                t_twin = psum.tile([P, NB], F32, name="t_twin", tag="B")
                nc.tensor.matmul(out=t_twin[:], lhsT=ones[:], rhs=rows, start=True, stop=True)

        def transpose_weight(raw, label):
            banks = []
            for half in range(2):
                bank = psum.tile([P, 2, 2, P], F32, name="%s_t%d" % (label, half), tag="B")
                for r in range(2):
                    words = raw[:, 2 * half + r, :].bitcast(F32).rearrange("p (q u) -> p u q", u=2)
                    for u in range(2):
                        nc.tensor.transpose(out=bank[:, r, u, :], in_=words[:, u, :], identity=ident[:])
                banks.append(bank)
            return banks

        w1_banks = transpose_weight(w1_raw, "w1")

        def empty_weight(banks, label):
            grouped = keep.tile([P, 4 * P * 4], BF16, name="%s_grouped" % label, align_bytes=64)
            words = grouped[:].bitcast(F32).rearrange("p (r m u) -> p r m u", r=4, u=2)
            for half in range(2):
                nc.scalar.copy(out=words[:, 2 * half : 2 * half + 2], in_=banks[half][:].rearrange("p r u m -> p r m u"))
            return grouped

        def quantise(src_flat, label):
            codes = keep.tile([P, 512], U32, name="%s_codes" % label, align_bytes=64)
            scales = keep.tile([P, 512], U8, name="%s_scales" % label, align_bytes=64)
            nc.vector.quantize_mx(out=codes[:].bitcast(FP8X4), scales=scales[:], in_=src_flat)
            return codes, scales

        sines = []

        def sine(c):
            s = keep.tile([P, 4, NB], F32, name="sine%d" % c)
            for j in range(4):
                nc.scalar.activation(
                    out=s[:, j, :], in_=t_all[c][:], func=ACT.Sin, bias=shift[:, j : j + 1], scale=neg_a[:, j : j + 1]
                )
            sines.append(s)

        emb_planes = {}

        def times_amp_t(c):
            ep = keep.tile([P, 4, NB], BF16, name="emb_planes%d" % c)
            t_for_vector = t_twin if c == 0 else t_all[c]
            for j in range(4):
                nc.vector.scalar_tensor_tensor(
                    out=ep[:, j, :], in0=sines[c][:, j, :], scalar=amp[:, j : j + 1], in1=t_for_vector[:], op0=ALU.mult, op1=ALU.mult
                )
            emb_planes[c] = ep

        def side_by_side(planes, label):
            grouped = keep.tile([P, NB, 4], BF16, name=label, align_bytes=64)
            nc.vector.tensor_copy(
                out=grouped[:].rearrange("p (c i) r -> p c r i", i=4), in_=planes[:].rearrange("p r (c i) -> p c r i", i=4)
            )
            return grouped

        emb = {}

        def regroup_emb(c):
            emb[c] = side_by_side(emb_planes[c], "emb%d" % c)

        emb_q = {}

        def quantise_emb(c):
            emb_q[c] = quantise(emb[c][:].rearrange("p b j -> p (b j)"), "emb%d" % c)

        z = {}

        def layer1(c, r):
            bank = psum.tile([P, NB], F32, name="z%d_%d" % (c, r), tag=("B" if c == 0 else "A"))
            cols = slice(r * P, (r + 1) * P)
            nc.tensor.matmul_mx(
                out=bank[:],
                lhsT=w1_q[0][:, cols].bitcast(FP8X4),
                lhsT_scale=w1_q[1][:, cols],
                rhs=emb_q[c][0][:].bitcast(FP8X4),
                rhs_scale=emb_q[c][1][:],
                start=True,
                stop=True,
            )
            z[(c, r)] = bank

        h_planes = {}

        def silu1(c):
            hp = keep.tile([P, 4, NB], BF16, name="h_planes%d" % c)
            for r in range(4):
                nc.scalar.activation(out=hp[:, r, :], in_=z[(c, r)][:], func=ACT.Silu, bias=b1_f[:, r : r + 1], scale=1.0)
            h_planes[c] = hp

        h_grouped = {}

        def regroup(c):
            h_grouped[c] = side_by_side(h_planes[c], "h_grouped%d" % c)

        h_q = {}

        def quantise_h(c):
            h_q[c] = quantise(h_grouped[c][:].rearrange("p b r -> p (b r)"), "h%d" % c)

        v = {}

        def layer2(c):
            for s in range(4):
                bank = psum.tile([P, O], F32, name="v%d_%d" % (c, s), tag="B")
                cols = slice(s * P, (s + 1) * P)
                nc.tensor.matmul_mx(
                    out=bank[:],
                    lhsT=h_q[c][0][:, cols].bitcast(FP8X4),
                    lhsT_scale=h_q[c][1][:, cols],
                    rhs=w2_q[0][:].bitcast(FP8X4),
                    rhs_scale=w2_q[1][:],
                    start=True,
                    stop=True,
                )
                v[(c, s)] = bank

        y = {}

        def add_bias2(c, pieces):
            if c not in y:
                y[c] = keep.tile([P, 4, O], F32, name="y%d" % c)
            for s in pieces:
                nc.vector.tensor_tensor(out=y[c][:, s, :], in0=v[(c, s)][:], in1=b2_all[:], op=ALU.add)

        def silu2_store(c):
            for s in range(4):
                nc.scalar.activation(out=y[c][:, s, :], in_=y[c][:, s, :], func=ACT.Silu)
                row = c * NB + s * P
                nc.sync.dma_start(out=out[row : row + P, :], in_=y[c][:, s, :])

        ALL = (0, 1, 2, 3)
        sine(0)
        w1_grouped = empty_weight(w1_banks, "w1")
        w2_banks = transpose_weight(w2_raw, "w2")
        sine(1)
        w2_grouped = empty_weight(w2_banks, "w2")
        sine(2)
        sine(3)
        times_amp_t(0)
        regroup_emb(0)
        times_amp_t(1)
        w1_q = quantise(w1_grouped[:], "w1")
        quantise_emb(0)
        for r in ALL:
            layer1(0, r)
        regroup_emb(1)
        b1_f = keep.tile([P, 4], F32, name="b1_f")
        nc.vector.tensor_copy(out=b1_f[:], in_=b1_raw[:])
        times_amp_t(2)
        w2_q = quantise(w2_grouped[:], "w2")
        quantise_emb(1)
        for r in (0, 1, 2):
            layer1(1, r)
        silu1(0)
        regroup_emb(2)
        times_amp_t(3)
        for r in (3,):
            layer1(1, r)
        quantise_emb(2)
        silu1(1)
        for r in ALL:
            layer1(2, r)
        regroup_emb(3)
        regroup(0)
        quantise_emb(3)
        quantise_h(0)
        layer2(0)
        silu1(2)
        for r in ALL:
            layer1(3, r)
        regroup(1)
        add_bias2(0, ALL)
        quantise_h(1)
        layer2(1)
        silu1(3)
        regroup(2)
        add_bias2(1, ALL)
        silu2_store(0)
        quantise_h(2)
        layer2(2)
        regroup(3)
        quantise_h(3)
        add_bias2(2, ALL)
        silu2_store(1)
        layer2(3)
        silu2_store(2)
        add_bias2(3, ALL)
        silu2_store(3)
